import numpy as np
import ml_dtypes


def mxq(x, axis, fmt="e4m3"):
    dtype, down = {"e4m3": (ml_dtypes.float8_e4m3fn, 7), "e5m2": (ml_dtypes.float8_e5m2, 14)}[fmt]
    v = np.moveaxis(np.asarray(x, np.float32).astype(ml_dtypes.bfloat16).astype(np.float64), axis, -1)
    blocks = v.reshape(v.shape[:-1] + (-1, 32))
    amax = np.abs(blocks).max(-1, keepdims=True)
    byte = np.maximum(np.where(amax > 0, np.frexp(amax)[1] - 1 + 127, 0) - down, 1)
    scale = np.exp2(byte - 127.0)
    codes = (blocks / scale).astype(np.float32).astype(dtype).astype(np.float64)
    return np.moveaxis((codes * scale).reshape(v.shape), -1, axis)


WIDE = False


def mx_kscale(k):
    if not WIDE:
        return np.ones(k)
    levels = np.array([10, -10, 5, -5, 0])
    if k % 512:
        return np.exp2(np.random.permutation(np.resize(levels, k // 32))).repeat(32)
    a = np.empty((k // 512, 16))
    for p in range(k // 512):
        a[p, :8] = np.random.permutation(np.resize(levels, 8))
        for g in range(8):
            far = levels[np.abs(levels - a[p, g]) >= 10]
            a[p, g + 8] = far[np.random.randint(len(far))]
    return np.exp2(a.ravel()).repeat(32)


BF16 = ml_dtypes.bfloat16


def bf(x):
    return np.asarray(x, np.float32).astype(BF16)


def f64(x):
    return np.asarray(x).astype(np.float64)


B, T, E, C, H, XB = 8, 1024, 512, 512, 4, 512
D = C // H
EPS = 1e-5


def silu(a):
    return a / (1.0 + np.exp(-a))


def setup_inputs():
    s, t = mx_kscale(E), mx_kscale(C)
    amp = 2.0 ** np.linspace(-8.0, 2.0, H)
    y = np.random.standard_normal((B, T, H, D)) * amp[None, None, :, None]
    return {"x": bf(np.random.standard_normal((B, T, E)) * s),
            "y_ret": bf(y.reshape(B, T, C)),
            "w_g": bf(np.random.standard_normal((E, C)) / np.sqrt(E) / s[:, None]),
            "w_proj": bf(np.random.standard_normal((C, E)) / np.sqrt(C) / t[:, None]),
            "gn_weight": bf((1.0 + 0.1 * np.random.standard_normal(C)) * t),
            "gn_bias": bf(0.1 * np.random.standard_normal(C) * t)}


def reference(x, y_ret, w_g, w_proj, gn_weight, gn_bias):
    yg = f64(y_ret).reshape(B * T, H, D)
    mu = yg.mean(axis=-1, keepdims=True)
    var = yg.var(axis=-1, keepdims=True)
    yn = (yg - mu) / np.sqrt(var + EPS)
    yn = yn.reshape(B * T, C) * f64(gn_weight)[None] + f64(gn_bias)[None]
    yn = yn.reshape(B, T, C)
    g = mxq(f64(x), 2, "e4m3") @ mxq(f64(w_g), 0, "e4m3")
    h = silu(g) * yn
    return mxq(h, 2, "e4m3") @ mxq(f64(w_proj), 0, "e4m3")

@@ -1,0 +1,239 @@
+from contextlib import ExitStack
+
+import concourse.mybir as mybir
+from concourse.masks import make_identity
+
+BF16 = mybir.dt.bfloat16
+F32 = mybir.dt.float32
+U32 = mybir.dt.uint32
+U8 = mybir.dt.uint8
+FP8X4 = mybir.dt.float8_e4m3fn_x4
+ACT = mybir.ActivationFunctionType
+ALU = mybir.AluOpType
+
+P = 128
+PACK = 4
+TOKENS = 8 * 1024
+WIDTH = 512
+HEADS = 4
+HEAD = WIDTH // HEADS
+QUARTER = HEAD // PACK
+TILES = 4
+BLOCK = TILES * P
+BLOCKS = TOKENS // BLOCK
+EPS = 1e-5
+LOAD_AHEAD = 3
+LAST_STAGE = 4
+WEIGHTS_STEP = 1
+VECTOR_BANKS = 0
+RUN = 4
+
+FLOPS = 2 * 2 * TOKENS * WIDTH * WIDTH
+
+
+def tile_multiscaleretention_pc_t_kernel(tc, x, y_ret, w_g, w_proj, gn_weight, gn_bias, out):
+    nc = tc.nc
+    x_blocks = x.flatten_outer_dims().rearrange("(n p j) e -> n p j e", p=P, j=TILES)
+    y_blocks = y_ret.flatten_outer_dims().rearrange("(n p j) c -> n p j c", p=P, j=TILES)
+    out_blocks = out.flatten_outer_dims().rearrange("(n p j) e -> n p j e", p=P, j=TILES)
+
+    with ExitStack() as ctx:
+        ctx.enter_context(tc.manual_schedule())
+        consts = ctx.enter_context(tc.tile_pool(name="consts", bufs=1))
+        loads = ctx.enter_context(tc.tile_pool(name="loads", bufs=LOAD_AHEAD + 3))
+        work = ctx.enter_context(tc.tile_pool(name="work", bufs=3))
+        psum = ctx.enter_context(tc.psum_pool(name="psum", bufs=8))
+        live = {}
+
+        def quantise(values, pool, name):
+            columns = values.shape[1] // PACK
+            codes = pool.tile([P, columns], U32, name=name + "_codes", align_bytes=64)
+            scales = pool.tile([P, columns], U8, name=name + "_scales", align_bytes=64)
+            nc.vector.quantize_mx(out=codes[:].bitcast(FP8X4), scales=scales[:], in_=values)
+            return codes, scales
+
+        def load(n):
+            y_sb = loads.tile([P, TILES, WIDTH], BF16, name="y_sb")
+            nc.sync.dma_start(out=y_sb[:], in_=y_blocks[n])
+            x_sb = loads.tile([P, TILES, WIDTH], BF16, name="x_sb")
+            nc.sync.dma_start(out=x_sb[:], in_=x_blocks[n])
+            live["x_sb", n] = x_sb
+            live["y_sb", n] = y_sb
+
+        def statistics(n):
+            y_sb = live["y_sb", n]
+            stats = work.tile([P, TILES * HEADS, 3], F32, name="stats")
+            for j in range(TILES):
+                for h in range(0, HEADS, 2):
+                    nc.vector.bn_stats(
+                        out=stats[:, j * HEADS + h : j * HEADS + h + 2, :].rearrange("p h s -> p (h s)"),
+                        in_=y_sb[:, j, h * HEAD : (h + 2) * HEAD].rearrange("p (h c) -> p c h", h=2),
+                    )
+            var_eps = work.tile([P, TILES * HEADS], F32, name="var_eps")
+            nc.gpsimd.tensor_scalar(
+                out=var_eps[:], in0=stats[:, :, 2], scalar1=1.0 / HEAD, scalar2=EPS, op0=ALU.mult, op1=ALU.add
+            )
+            rstd = work.tile([P, TILES * HEADS], F32, name="rstd")
+            nc.gpsimd.tensor_tensor(out=rstd[:], in0=var_eps[:], in1=minus_half[:], op=ALU.pow)
+            live["stats", n] = stats
+            live["rstd", n] = rstd
+
+        def centre_and_scale(n):
+            y_sb, stats, rstd = live["y_sb", n], live["stats", n], live["rstd", n]
+            z = work.tile([P, TILES, PACK, P], F32, name="z")
+            for j in range(TILES):
+                for h in range(HEADS):
+                    i = j * HEADS + h
+                    nc.vector.tensor_scalar(
+                        out=z[:, j, :, h * QUARTER : (h + 1) * QUARTER].rearrange("p t (c i) -> p c t i", i=RUN),
+                        in0=y_sb[:, j, h * HEAD : (h + 1) * HEAD].rearrange("p (c i t) -> p c t i", i=RUN, t=PACK),
+                        scalar1=stats[:, i, 1:2],
+                        scalar2=rstd[:, i : i + 1],
+                        op0=ALU.subtract,
+                        op1=ALU.mult,
+                    )
+            live["z", n] = z
+
+        def affine(n):
+            z = live["z", n]
+            yn = work.tile([P, PACK, BLOCK], F32, name="yn")
+            for t in range(PACK):
+                zT = psum.tile([P, TILES, P], F32, name="zT", tag="bank")
+                for j in range(TILES):
+                    nc.tensor.transpose(zT[:, j, :], z[:, j, t, :], ident_f32[:])
+                nc.scalar.activation(
+                    out=yn[:, t, :],
+                    in_=zT[:].rearrange("p j w -> p (j w)"),
+                    func=ACT.Identity,
+                    scale=gain[:, t : t + 1],
+                    bias=bias[:, t : t + 1],
+                )
+            live["yn", n] = yn
+
+        def transpose_tokens(n):
+            x_sb = live["x_sb", n]
+            x_grouped = work.tile([P, BLOCK * PACK], BF16, name="x_grouped", align_bytes=64)
+            x_words = x_grouped[:].bitcast(F32).rearrange("p (j w u) -> p j w u", j=TILES, u=2)
+            for half in range(TILES // 2):
+                xT = psum.tile([P, 2, 2, P], F32, name="xT", tag="bank")
+                for j in range(2):
+                    for u in range(2):
+                        nc.tensor.transpose(
+                            xT[:, j, u, :],
+                            x_sb[:, 2 * half + j, :].bitcast(F32)[:, u : 2 * P : 2],
+                            ident_f32[:],
+                        )
+                nc.scalar.copy(
+                    out=x_words[:, 2 * half : 2 * half + 2], in_=xT[:].rearrange("p j u w -> p j w u")
+                )
+            live["x_grouped", n] = x_grouped
+
+        def quantise_tokens(n):
+            live["x_mx", n] = quantise(live["x_grouped", n][:], work, "x")
+
+        def gate(n):
+            x_codes, x_scales = live["x_mx", n]
+            wg_codes, wg_scales = live["wg_mx"]
+            gated = work.tile([P, TILES, P // RUN, HEADS, RUN], F32, name="gated")
+            for j in range(TILES):
+                g_ps = psum.tile([P, HEADS, P], F32, name="g_ps", tag="bank")
+                for h in range(HEADS):
+                    nc.tensor.matmul_mx(
+                        out=g_ps[:, h, :],
+                        lhsT=wg_codes[:, h * HEAD : (h + 1) * HEAD].bitcast(FP8X4),
+                        lhsT_scale=wg_scales[:, h * HEAD : (h + 1) * HEAD],
+                        rhs=x_codes[:, j * P : (j + 1) * P].bitcast(FP8X4),
+                        rhs_scale=x_scales[:, j * P : (j + 1) * P],
+                        start=True,
+                        stop=True,
+                    )
+                nc.scalar.activation(
+                    out=gated[:, j], in_=g_ps[:].rearrange("p h (c i) -> p c h i", i=RUN), func=ACT.Silu
+                )
+            live["gated", n] = gated
+
+        def multiply(n):
+            hidden = work.tile([P, BLOCK, PACK], BF16, name="hidden", align_bytes=64)
+            nc.vector.tensor_tensor(
+                out=hidden[:].rearrange("p (c i) h -> p c h i", i=RUN),
+                in0=live["gated", n][:].rearrange("p j c h i -> p (j c) h i"),
+                in1=live["yn", n][:].rearrange("p h (c i) -> p c h i", i=RUN),
+                op=ALU.mult,
+            )
+            live["hidden", n] = hidden
+
+        def quantise_hidden(n):
+            live["h_mx", n] = quantise(live["hidden", n][:].rearrange("p n h -> p (n h)"), work, "h")
+
+        def project(n):
+            h_codes, h_scales = live["h_mx", n]
+            wp_codes, wp_scales = live["wp_mx"]
+            out_sb = work.tile([P, TILES, WIDTH], F32, name="out_sb")
+            for j in range(TILES):
+                o_ps = psum.tile([P, WIDTH], F32, name="o_ps", tag="bank")
+                nc.tensor.matmul_mx(
+                    out=o_ps[:],
+                    lhsT=h_codes[:, j * P : (j + 1) * P].bitcast(FP8X4),
+                    lhsT_scale=h_scales[:, j * P : (j + 1) * P],
+                    rhs=wp_codes[:].bitcast(FP8X4),
+                    rhs_scale=wp_scales[:],
+                    start=True,
+                    stop=True,
+                )
+                if j < VECTOR_BANKS:
+                    nc.vector.tensor_copy(out=out_sb[:, j, :], in_=o_ps[:])
+                else:
+                    nc.scalar.copy(out=out_sb[:, j, :], in_=o_ps[:])
+                nc.sync.dma_start(out=out_blocks[n][:, j, :], in_=out_sb[:, j, :])
+
+        def prepare_weights():
+            wg_grouped = consts.tile([P, WIDTH, PACK], BF16, name="wg_grouped", align_bytes=64)
+            nc.vector.tensor_copy(
+                out=wg_grouped[:].rearrange("p (t m) k -> p t m k", t=PACK),
+                in_=wg_raw[:].rearrange("p k (m t) -> p t m k", t=PACK),
+            )
+            wp_grouped = consts.tile([P, WIDTH, PACK], BF16, name="wp_grouped", align_bytes=64)
+            nc.vector.tensor_copy(out=wp_grouped[:], in_=wp_raw[:].rearrange("p t c -> p c t"))
+            live["wg_mx"] = quantise(wg_grouped[:].rearrange("p c t -> p (c t)"), consts, "wg")
+            live["wp_mx"] = quantise(wp_grouped[:].rearrange("p c t -> p (c t)"), consts, "wp")
+            nc.vector.tensor_copy(out=gain[:], in_=gain_raw[:])
+            nc.vector.tensor_copy(out=bias[:], in_=bias_raw[:])
+
+        load(0)
+        wg_raw = consts.tile([P, PACK, WIDTH], BF16, name="wg_raw")
+        nc.sync.dma_start(out=wg_raw[:], in_=w_g.rearrange("(p k) c -> p k c", k=PACK))
+        gain_raw = consts.tile([P, PACK], BF16, name="gain_raw")
+        nc.sync.dma_start(out=gain_raw[:], in_=gn_weight.rearrange("(p t) -> p t", t=PACK))
+        bias_raw = consts.tile([P, PACK], BF16, name="bias_raw")
+        nc.sync.dma_start(out=bias_raw[:], in_=gn_bias.rearrange("(p t) -> p t", t=PACK))
+        wp_raw = consts.tile([P, PACK, WIDTH], BF16, name="wp_raw")
+        nc.sync.dma_start(out=wp_raw[:], in_=w_proj.rearrange("(p t) n -> p t n", t=PACK))
+        for n in range(1, LOAD_AHEAD):
+            load(n)
+
+        ident_f32 = consts.tile([P, P], F32, name="ident_f32")
+        make_identity(nc, ident_f32[:])
+        minus_half = consts.tile([P, TILES * HEADS], F32, name="minus_half")
+        nc.vector.memset(minus_half[:], -0.5)
+        gain = consts.tile([P, PACK], F32, name="gain")
+        bias = consts.tile([P, PACK], F32, name="bias")
+        table_warmer = consts.tile([P, 1], F32, name="table_warmer")
+        nc.scalar.activation(out=table_warmer[:], in_=minus_half[:, 0:1], func=ACT.Silu)
+
+        def run(stage, n):
+            if 0 <= n < BLOCKS:
+                stage(n)
+
+        for step in range(BLOCKS + LAST_STAGE):
+            run(quantise_tokens, step - 1)
+            if step == WEIGHTS_STEP:
+                prepare_weights()
+            run(multiply, step - 3)
+            run(project, step - 4)
+            run(quantise_hidden, step - 3)
+            run(statistics, step)
+            run(centre_and_scale, step - 1)
+            run(gate, step - 2)
+            run(affine, step - 2)
+            run(transpose_tokens, step)
+            run(load, step + LOAD_AHEAD)

@@ -18,202 +18,240 @@ WIDTH = 512
 HEADS = 4
 HEAD = WIDTH // HEADS
 QUARTER = HEAD // PACK
-TILES = 4
-BLOCK = TILES * P
-BLOCKS = TOKENS // BLOCK
 EPS = 1e-5
+RUN = 4
+MAX_TILES = 4
+MAX_TOKENS = MAX_TILES * P
+MAX_PAIRS = MAX_TILES * HEADS
+TILES = [2] + [MAX_TILES] * 15 + [2]
+STARTS = [sum(TILES[:n]) for n in range(len(TILES))]
+GROUPS = len(TILES)
 LOAD_AHEAD = 3
 LAST_STAGE = 4
-WEIGHTS_STEP = 1
-VECTOR_BANKS = 0
-RUN = 4
+VECTOR_SLOTS = 2
+CENTRED_FIRST = 4
 
 FLOPS = 2 * 2 * TOKENS * WIDTH * WIDTH
 
 
 def tile_multiscaleretention_pc_t_kernel(tc, x, y_ret, w_g, w_proj, gn_weight, gn_bias, out):
     nc = tc.nc
-    x_blocks = x.flatten_outer_dims().rearrange("(n p j) e -> n p j e", p=P, j=TILES)
-    y_blocks = y_ret.flatten_outer_dims().rearrange("(n p j) c -> n p j c", p=P, j=TILES)
-    out_blocks = out.flatten_outer_dims().rearrange("(n p j) e -> n p j e", p=P, j=TILES)
+
+    def rows_of(tensor, n):
+        rows = tensor.flatten_outer_dims()[P * STARTS[n] : P * (STARTS[n] + TILES[n]), :]
+        return rows.rearrange("(p j) e -> p j e", p=P)
 
     with ExitStack() as ctx:
         ctx.enter_context(tc.manual_schedule())
         consts = ctx.enter_context(tc.tile_pool(name="consts", bufs=1))
         loads = ctx.enter_context(tc.tile_pool(name="loads", bufs=LOAD_AHEAD + 3))
         work = ctx.enter_context(tc.tile_pool(name="work", bufs=3))
-        psum = ctx.enter_context(tc.psum_pool(name="psum", bufs=8))
+        psum = ctx.enter_context(tc.psum_pool(name="psum", bufs=8 - VECTOR_SLOTS))
+        psum_vector = ctx.enter_context(tc.psum_pool(name="psum_vector", bufs=VECTOR_SLOTS))
         live = {}
 
         def quantise(values, pool, name):
             columns = values.shape[1] // PACK
-            codes = pool.tile([P, columns], U32, name=name + "_codes", align_bytes=64)
-            scales = pool.tile([P, columns], U8, name=name + "_scales", align_bytes=64)
-            nc.vector.quantize_mx(out=codes[:].bitcast(FP8X4), scales=scales[:], in_=values)
+            codes = pool.tile([P, WIDTH], U32, name=name + "_codes", align_bytes=64)
+            scales = pool.tile([P, WIDTH], U8, name=name + "_scales", align_bytes=64)
+            nc.vector.quantize_mx(
+                out=codes[:, 0:columns].bitcast(FP8X4), scales=scales[:, 0:columns], in_=values
+            )
             return codes, scales
 
-        def load(n):
-            y_sb = loads.tile([P, TILES, WIDTH], BF16, name="y_sb")
-            nc.sync.dma_start(out=y_sb[:], in_=y_blocks[n])
-            x_sb = loads.tile([P, TILES, WIDTH], BF16, name="x_sb")
-            nc.sync.dma_start(out=x_sb[:], in_=x_blocks[n])
-            live["x_sb", n] = x_sb
+        def load_y(n):
+            y_sb = loads.tile([P, MAX_TILES, WIDTH], BF16, name="y_sb")
+            nc.sync.dma_start(out=y_sb[:, 0 : TILES[n], :], in_=rows_of(y_ret, n))
             live["y_sb", n] = y_sb
+
+        def load_x(n):
+            x_sb = loads.tile([P, MAX_TILES, WIDTH], BF16, name="x_sb")
+            nc.sync.dma_start(out=x_sb[:, 0 : TILES[n], :], in_=rows_of(x, n))
+            live["x_sb", n] = x_sb
+
+        def load(n):
+            load_y(n)
+            load_x(n)
 
         def statistics(n):
             y_sb = live["y_sb", n]
-            stats = work.tile([P, TILES * HEADS, 3], F32, name="stats")
-            for j in range(TILES):
+            stats = work.tile([P, MAX_PAIRS, 3], F32, name="stats")
+            for j in range(TILES[n]):
                 for h in range(0, HEADS, 2):
                     nc.vector.bn_stats(
                         out=stats[:, j * HEADS + h : j * HEADS + h + 2, :].rearrange("p h s -> p (h s)"),
                         in_=y_sb[:, j, h * HEAD : (h + 2) * HEAD].rearrange("p (h c) -> p c h", h=2),
                     )
-            var_eps = work.tile([P, TILES * HEADS], F32, name="var_eps")
-            nc.gpsimd.tensor_scalar(
-                out=var_eps[:], in0=stats[:, :, 2], scalar1=1.0 / HEAD, scalar2=EPS, op0=ALU.mult, op1=ALU.add
-            )
-            rstd = work.tile([P, TILES * HEADS], F32, name="rstd")
-            nc.gpsimd.tensor_tensor(out=rstd[:], in0=var_eps[:], in1=minus_half[:], op=ALU.pow)
             live["stats", n] = stats
+
+        def inverse_roots(n):
+            pairs = TILES[n] * HEADS
+            var_eps = work.tile([P, MAX_PAIRS], F32, name="var_eps")
+            nc.vector.tensor_scalar(
+                out=var_eps[:, 0:pairs],
+                in0=live["stats", n][:, 0:pairs, 2],
+                scalar1=1.0 / HEAD,
+                scalar2=EPS,
+                op0=ALU.mult,
+                op1=ALU.add,
+            )
+            rstd = work.tile([P, MAX_PAIRS], F32, name="rstd")
+            nc.gpsimd.tensor_tensor(
+                out=rstd[:, 0:pairs], in0=var_eps[:, 0:pairs], in1=minus_half[:, 0:pairs], op=ALU.pow
+            )
             live["rstd", n] = rstd
 
         def centre_and_scale(n):
             y_sb, stats, rstd = live["y_sb", n], live["stats", n], live["rstd", n]
-            z = work.tile([P, TILES, PACK, P], F32, name="z")
-            for j in range(TILES):
+            z = work.tile([P, MAX_TILES, PACK, P], F32, name="z")
+            for j in range(TILES[n]):
                 for h in range(HEADS):
                     i = j * HEADS + h
+                    head = slice(h * HEAD, (h + 1) * HEAD)
+                    quarter = slice(h * QUARTER, (h + 1) * QUARTER)
                     nc.vector.tensor_scalar(
-                        out=z[:, j, :, h * QUARTER : (h + 1) * QUARTER].rearrange("p t (c i) -> p c t i", i=RUN),
-                        in0=y_sb[:, j, h * HEAD : (h + 1) * HEAD].rearrange("p (c i t) -> p c t i", i=RUN, t=PACK),
+                        out=z[:, j, :, quarter].rearrange("p t (c i) -> p c t i", i=RUN),
+                        in0=y_sb[:, j, head].rearrange("p (c i t) -> p c t i", i=RUN, t=PACK),
                         scalar1=stats[:, i, 1:2],
                         scalar2=rstd[:, i : i + 1],
                         op0=ALU.subtract,
                         op1=ALU.mult,
                     )
+                    if i == CENTRED_FIRST - 1:
+                        run(inverse_roots, n + 1)
             live["z", n] = z
 
         def affine(n):
             z = live["z", n]
-            yn = work.tile([P, PACK, BLOCK], F32, name="yn")
-            for t in range(PACK):
-                zT = psum.tile([P, TILES, P], F32, name="zT", tag="bank")
-                for j in range(TILES):
-                    nc.tensor.transpose(zT[:, j, :], z[:, j, t, :], ident_f32[:])
-                nc.scalar.activation(
-                    out=yn[:, t, :],
-                    in_=zT[:].rearrange("p j w -> p (j w)"),
-                    func=ACT.Identity,
-                    scale=gain[:, t : t + 1],
-                    bias=bias[:, t : t + 1],
-                )
+            yn = work.tile([P, PACK, MAX_TOKENS], F32, name="yn")
             live["yn", n] = yn
+            live["vector_banks", n] = []
+            for t in range(PACK):
+                on_vector = n == GROUPS - 1 and t >= PACK - VECTOR_SLOTS
+                if on_vector:
+                    zT = psum_vector.tile([P, MAX_TILES, P], F32, name="zT_vector", tag="bank_vector")
+                else:
+                    zT = psum.tile([P, MAX_TILES, P], F32, name="zT", tag="bank")
+                for j in range(TILES[n]):
+                    nc.tensor.transpose(zT[:, j, :], z[:, j, t, :], ident_f32[:])
+                if on_vector:
+                    live["vector_banks", n].append((t, zT))
+                else:
+                    nc.scalar.activation(
+                        out=yn[:, t, 0 : TILES[n] * P],
+                        in_=zT[:, 0 : TILES[n], :].rearrange("p j w -> p (j w)"),
+                        func=ACT.Identity,
+                        scale=gain[:, t : t + 1],
+                        bias=bias[:, t : t + 1],
+                    )
+
+        def affine_on_vector(n):
+            for t, zT in live["vector_banks", n]:
+                nc.vector.tensor_scalar(
+                    out=live["yn", n][:, t, 0 : TILES[n] * P],
+                    in0=zT[:, 0 : TILES[n], :].rearrange("p j w -> p (j w)"),
+                    scalar1=gain[:, t : t + 1],
+                    scalar2=bias[:, t : t + 1],
+                    op0=ALU.mult,
+                    op1=ALU.add,
+                )
 
         def transpose_tokens(n):
             x_sb = live["x_sb", n]
-            x_grouped = work.tile([P, BLOCK * PACK], BF16, name="x_grouped", align_bytes=64)
-            x_words = x_grouped[:].bitcast(F32).rearrange("p (j w u) -> p j w u", j=TILES, u=2)
-            for half in range(TILES // 2):
+            x_grouped = work.tile([P, MAX_TOKENS * PACK], BF16, name="x_grouped", align_bytes=64)
+            x_words = x_grouped[:].bitcast(F32).rearrange("p (j w u) -> p j w u", j=MAX_TILES, u=2)
+            for first in range(0, TILES[n], 2):
                 xT = psum.tile([P, 2, 2, P], F32, name="xT", tag="bank")
                 for j in range(2):
                     for u in range(2):
                         nc.tensor.transpose(
-                            xT[:, j, u, :],
-                            x_sb[:, 2 * half + j, :].bitcast(F32)[:, u : 2 * P : 2],
-                            ident_f32[:],
+                            xT[:, j, u, :], x_sb[:, first + j, :].bitcast(F32)[:, u : 2 * P : 2], ident_f32[:]
                         )
-                nc.scalar.copy(
-                    out=x_words[:, 2 * half : 2 * half + 2], in_=xT[:].rearrange("p j u w -> p j w u")
-                )
+                nc.scalar.copy(out=x_words[:, first : first + 2], in_=xT[:].rearrange("p j u w -> p j w u"))
             live["x_grouped", n] = x_grouped
 
         def quantise_tokens(n):
-            live["x_mx", n] = quantise(live["x_grouped", n][:], work, "x")
+            live["x_mx", n] = quantise(live["x_grouped", n][:, 0 : TILES[n] * P * PACK], work, "x")
 
         def gate(n):
             x_codes, x_scales = live["x_mx", n]
             wg_codes, wg_scales = live["wg_mx"]
-            gated = work.tile([P, TILES, P // RUN, HEADS, RUN], F32, name="gated")
-            for j in range(TILES):
-                g_ps = psum.tile([P, HEADS, P], F32, name="g_ps", tag="bank")
-                for h in range(HEADS):
+            gated = work.tile([P, MAX_TILES, P // RUN, PACK, RUN], F32, name="gated")
+            for j in range(TILES[n]):
+                tokens = slice(j * P, (j + 1) * P)
+                g_ps = psum.tile([P, PACK, P], F32, name="g_ps", tag="bank")
+                for t in range(PACK):
+                    slot = slice(t * P, (t + 1) * P)
                     nc.tensor.matmul_mx(
-                        out=g_ps[:, h, :],
-                        lhsT=wg_codes[:, h * HEAD : (h + 1) * HEAD].bitcast(FP8X4),
-                        lhsT_scale=wg_scales[:, h * HEAD : (h + 1) * HEAD],
-                        rhs=x_codes[:, j * P : (j + 1) * P].bitcast(FP8X4),
-                        rhs_scale=x_scales[:, j * P : (j + 1) * P],
+                        out=g_ps[:, t, :],
+                        lhsT=wg_codes[:, slot].bitcast(FP8X4),
+                        lhsT_scale=wg_scales[:, slot],
+                        rhs=x_codes[:, tokens].bitcast(FP8X4),
+                        rhs_scale=x_scales[:, tokens],
                         start=True,
                         stop=True,
                     )
                 nc.scalar.activation(
-                    out=gated[:, j], in_=g_ps[:].rearrange("p h (c i) -> p c h i", i=RUN), func=ACT.Silu
+                    out=gated[:, j], in_=g_ps[:].rearrange("p t (c i) -> p c t i", i=RUN), func=ACT.Silu
                 )
             live["gated", n] = gated
 
         def multiply(n):
-            hidden = work.tile([P, BLOCK, PACK], BF16, name="hidden", align_bytes=64)
+            hidden = work.tile([P, MAX_TOKENS, PACK], BF16, name="hidden", align_bytes=64)
+            tokens = slice(0, TILES[n] * P)
             nc.vector.tensor_tensor(
-                out=hidden[:].rearrange("p (c i) h -> p c h i", i=RUN),
-                in0=live["gated", n][:].rearrange("p j c h i -> p (j c) h i"),
-                in1=live["yn", n][:].rearrange("p h (c i) -> p c h i", i=RUN),
+                out=hidden[:, tokens, :].rearrange("p (c i) t -> p c t i", i=RUN),
+                in0=live["gated", n][:, 0 : TILES[n]].rearrange("p j c t i -> p (j c) t i"),
+                in1=live["yn", n][:, :, tokens].rearrange("p t (c i) -> p c t i", i=RUN),
                 op=ALU.mult,
             )
             live["hidden", n] = hidden
 
         def quantise_hidden(n):
-            live["h_mx", n] = quantise(live["hidden", n][:].rearrange("p n h -> p (n h)"), work, "h")
+            hidden = live["hidden", n][:, 0 : TILES[n] * P, :]
+            live["h_mx", n] = quantise(hidden.rearrange("p w t -> p (w t)"), work, "h")
 
         def project(n):
             h_codes, h_scales = live["h_mx", n]
             wp_codes, wp_scales = live["wp_mx"]
-            out_sb = work.tile([P, TILES, WIDTH], F32, name="out_sb")
-            for j in range(TILES):
+            out_sb = work.tile([P, MAX_TILES, WIDTH], F32, name="out_sb")
+            for j in range(TILES[n]):
+                tokens = slice(j * P, (j + 1) * P)
                 o_ps = psum.tile([P, WIDTH], F32, name="o_ps", tag="bank")
                 nc.tensor.matmul_mx(
                     out=o_ps[:],
-                    lhsT=h_codes[:, j * P : (j + 1) * P].bitcast(FP8X4),
-                    lhsT_scale=h_scales[:, j * P : (j + 1) * P],
+                    lhsT=h_codes[:, tokens].bitcast(FP8X4),
+                    lhsT_scale=h_scales[:, tokens],
                     rhs=wp_codes[:].bitcast(FP8X4),
                     rhs_scale=wp_scales[:],
                     start=True,
                     stop=True,
                 )
-                if j < VECTOR_BANKS:
+                if n == GROUPS - 1 and j % 2 == 1:
                     nc.vector.tensor_copy(out=out_sb[:, j, :], in_=o_ps[:])
                 else:
                     nc.scalar.copy(out=out_sb[:, j, :], in_=o_ps[:])
-                nc.sync.dma_start(out=out_blocks[n][:, j, :], in_=out_sb[:, j, :])
-
-        def prepare_weights():
-            wg_grouped = consts.tile([P, WIDTH, PACK], BF16, name="wg_grouped", align_bytes=64)
-            nc.vector.tensor_copy(
-                out=wg_grouped[:].rearrange("p (t m) k -> p t m k", t=PACK),
-                in_=wg_raw[:].rearrange("p k (m t) -> p t m k", t=PACK),
-            )
-            wp_grouped = consts.tile([P, WIDTH, PACK], BF16, name="wp_grouped", align_bytes=64)
-            nc.vector.tensor_copy(out=wp_grouped[:], in_=wp_raw[:].rearrange("p t c -> p c t"))
-            live["wg_mx"] = quantise(wg_grouped[:].rearrange("p c t -> p (c t)"), consts, "wg")
-            live["wp_mx"] = quantise(wp_grouped[:].rearrange("p c t -> p (c t)"), consts, "wp")
-            nc.vector.tensor_copy(out=gain[:], in_=gain_raw[:])
-            nc.vector.tensor_copy(out=bias[:], in_=bias_raw[:])
+                nc.sync.dma_start(out=rows_of(out, n)[:, j, :], in_=out_sb[:, j, :])
 
         load(0)
         wg_raw = consts.tile([P, PACK, WIDTH], BF16, name="wg_raw")
-        nc.sync.dma_start(out=wg_raw[:], in_=w_g.rearrange("(p k) c -> p k c", k=PACK))
+        nc.sync.dma_start(out=wg_raw[:], in_=w_g.rearrange("(p t) c -> p t c", t=PACK))
+        load_x(1)
         gain_raw = consts.tile([P, PACK], BF16, name="gain_raw")
         nc.sync.dma_start(out=gain_raw[:], in_=gn_weight.rearrange("(p t) -> p t", t=PACK))
         bias_raw = consts.tile([P, PACK], BF16, name="bias_raw")
         nc.sync.dma_start(out=bias_raw[:], in_=gn_bias.rearrange("(p t) -> p t", t=PACK))
+        load_y(1)
         wp_raw = consts.tile([P, PACK, WIDTH], BF16, name="wp_raw")
-        nc.sync.dma_start(out=wp_raw[:], in_=w_proj.rearrange("(p t) n -> p t n", t=PACK))
-        for n in range(1, LOAD_AHEAD):
+        nc.sync.dma_start(out=wp_raw[:], in_=w_proj.rearrange("(p t) c -> p t c", t=PACK))
+        for n in range(2, LOAD_AHEAD):
             load(n)
+        wg_grouped = consts.tile([P, WIDTH, PACK], BF16, name="wg_grouped", align_bytes=64)
+        wp_grouped = consts.tile([P, WIDTH, PACK], BF16, name="wp_grouped", align_bytes=64)
 
         ident_f32 = consts.tile([P, P], F32, name="ident_f32")
         make_identity(nc, ident_f32[:])
-        minus_half = consts.tile([P, TILES * HEADS], F32, name="minus_half")
+        minus_half = consts.tile([P, MAX_PAIRS], F32, name="minus_half")
         nc.vector.memset(minus_half[:], -0.5)
         gain = consts.tile([P, PACK], F32, name="gain")
         bias = consts.tile([P, PACK], F32, name="bias")
@@ -221,19 +259,32 @@ def tile_multiscaleretention_pc_t_kernel(tc, x, y_ret, w_g, w_proj, gn_weight, g
         nc.scalar.activation(out=table_warmer[:], in_=minus_half[:, 0:1], func=ACT.Silu)
 
         def run(stage, n):
-            if 0 <= n < BLOCKS:
+            if 0 <= n < GROUPS:
                 stage(n)
 
-        for step in range(BLOCKS + LAST_STAGE):
+        for step in range(GROUPS + LAST_STAGE):
+            run(affine_on_vector, step - 3)
             run(quantise_tokens, step - 1)
-            if step == WEIGHTS_STEP:
-                prepare_weights()
+            if step == 1:
+                nc.vector.tensor_copy(
+                    out=wg_grouped[:].rearrange("p (t m) k -> p t m k", t=PACK),
+                    in_=wg_raw[:].rearrange("p k (m t) -> p t m k", t=PACK),
+                )
+                live["wg_mx"] = quantise(wg_grouped[:].rearrange("p c k -> p (c k)"), consts, "wg")
+                nc.vector.tensor_copy(out=gain[:], in_=gain_raw[:])
+                nc.vector.tensor_copy(out=bias[:], in_=bias_raw[:])
             run(multiply, step - 3)
             run(project, step - 4)
             run(quantise_hidden, step - 3)
             run(statistics, step)
+            if step == 0:
+                inverse_roots(0)
             run(centre_and_scale, step - 1)
+            if step == 2:
+                live["wp_mx"] = quantise(wp_grouped[:].rearrange("p c k -> p (c k)"), consts, "wp")
             run(gate, step - 2)
             run(affine, step - 2)
             run(transpose_tokens, step)
+            if step == 1:
+                nc.scalar.copy(out=wp_grouped[:], in_=wp_raw[:].rearrange("p k c -> p c k"))
             run(load, step + LOAD_AHEAD)

from contextlib import ExitStack

import concourse.mybir as mybir
from concourse.masks import make_identity

BF16 = mybir.dt.bfloat16
F32 = mybir.dt.float32
U32 = mybir.dt.uint32
U8 = mybir.dt.uint8
FP8X4 = mybir.dt.float8_e4m3fn_x4
ACT = mybir.ActivationFunctionType
ALU = mybir.AluOpType

P = 128
PACK = 4
TOKENS = 8 * 1024
WIDTH = 512
HEADS = 4
HEAD = WIDTH // HEADS
QUARTER = HEAD // PACK
EPS = 1e-5
RUN = 4
MAX_TILES = 4
MAX_TOKENS = MAX_TILES * P
MAX_PAIRS = MAX_TILES * HEADS
TILES = [2] + [MAX_TILES] * 15 + [2]
STARTS = [sum(TILES[:n]) for n in range(len(TILES))]
GROUPS = len(TILES)
LOAD_AHEAD = 3
LAST_STAGE = 4
VECTOR_SLOTS = 2
CENTRED_FIRST = 4

FLOPS = 2 * 2 * TOKENS * WIDTH * WIDTH


def tile_multiscaleretention_pc_t_kernel(tc, x, y_ret, w_g, w_proj, gn_weight, gn_bias, out):
    nc = tc.nc

    def rows_of(tensor, n):
        rows = tensor.flatten_outer_dims()[P * STARTS[n] : P * (STARTS[n] + TILES[n]), :]
        return rows.rearrange("(p j) e -> p j e", p=P)

    with ExitStack() as ctx:
        ctx.enter_context(tc.manual_schedule())
        consts = ctx.enter_context(tc.tile_pool(name="consts", bufs=1))
        loads = ctx.enter_context(tc.tile_pool(name="loads", bufs=LOAD_AHEAD + 3))
        work = ctx.enter_context(tc.tile_pool(name="work", bufs=3))
        psum = ctx.enter_context(tc.psum_pool(name="psum", bufs=8 - VECTOR_SLOTS))
        psum_vector = ctx.enter_context(tc.psum_pool(name="psum_vector", bufs=VECTOR_SLOTS))
        live = {}

        def quantise(values, pool, name):
            columns = values.shape[1] // PACK
            codes = pool.tile([P, WIDTH], U32, name=name + "_codes", align_bytes=64)
            scales = pool.tile([P, WIDTH], U8, name=name + "_scales", align_bytes=64)
            nc.vector.quantize_mx(
                out=codes[:, 0:columns].bitcast(FP8X4), scales=scales[:, 0:columns], in_=values
            )
            return codes, scales

        def load_y(n):
            y_sb = loads.tile([P, MAX_TILES, WIDTH], BF16, name="y_sb")
            nc.sync.dma_start(out=y_sb[:, 0 : TILES[n], :], in_=rows_of(y_ret, n))
            live["y_sb", n] = y_sb

        def load_x(n):
            x_sb = loads.tile([P, MAX_TILES, WIDTH], BF16, name="x_sb")
            nc.sync.dma_start(out=x_sb[:, 0 : TILES[n], :], in_=rows_of(x, n))
            live["x_sb", n] = x_sb

        def load(n):
            load_y(n)
            load_x(n)

        def statistics(n):
            y_sb = live["y_sb", n]
            stats = work.tile([P, MAX_PAIRS, 3], F32, name="stats")
            for j in range(TILES[n]):
                for h in range(0, HEADS, 2):
                    nc.vector.bn_stats(
                        out=stats[:, j * HEADS + h : j * HEADS + h + 2, :].rearrange("p h s -> p (h s)"),
                        in_=y_sb[:, j, h * HEAD : (h + 2) * HEAD].rearrange("p (h c) -> p c h", h=2),
                    )
            live["stats", n] = stats

        def inverse_roots(n):
            pairs = TILES[n] * HEADS
            var_eps = work.tile([P, MAX_PAIRS], F32, name="var_eps")
            nc.vector.tensor_scalar(
                out=var_eps[:, 0:pairs],
                in0=live["stats", n][:, 0:pairs, 2],
                scalar1=1.0 / HEAD,
                scalar2=EPS,
                op0=ALU.mult,
                op1=ALU.add,
            )
            rstd = work.tile([P, MAX_PAIRS], F32, name="rstd")
            nc.gpsimd.tensor_tensor(
                out=rstd[:, 0:pairs], in0=var_eps[:, 0:pairs], in1=minus_half[:, 0:pairs], op=ALU.pow
            )
            live["rstd", n] = rstd

        def centre_and_scale(n):
            y_sb, stats, rstd = live["y_sb", n], live["stats", n], live["rstd", n]
            z = work.tile([P, MAX_TILES, PACK, P], F32, name="z")
            for j in range(TILES[n]):
                for h in range(HEADS):
                    i = j * HEADS + h
                    head = slice(h * HEAD, (h + 1) * HEAD)
                    quarter = slice(h * QUARTER, (h + 1) * QUARTER)
                    nc.vector.tensor_scalar(
                        out=z[:, j, :, quarter].rearrange("p t (c i) -> p c t i", i=RUN),
                        in0=y_sb[:, j, head].rearrange("p (c i t) -> p c t i", i=RUN, t=PACK),
                        scalar1=stats[:, i, 1:2],
                        scalar2=rstd[:, i : i + 1],
                        op0=ALU.subtract,
                        op1=ALU.mult,
                    )
                    if i == CENTRED_FIRST - 1:
                        run(inverse_roots, n + 1)
            live["z", n] = z

        def affine(n):
            z = live["z", n]
            yn = work.tile([P, PACK, MAX_TOKENS], F32, name="yn")
            live["yn", n] = yn
            live["vector_banks", n] = []
            for t in range(PACK):
                on_vector = n == GROUPS - 1 and t >= PACK - VECTOR_SLOTS
                if on_vector:
                    zT = psum_vector.tile([P, MAX_TILES, P], F32, name="zT_vector", tag="bank_vector")
                else:
                    zT = psum.tile([P, MAX_TILES, P], F32, name="zT", tag="bank")
                for j in range(TILES[n]):
                    nc.tensor.transpose(zT[:, j, :], z[:, j, t, :], ident_f32[:])
                if on_vector:
                    live["vector_banks", n].append((t, zT))
                else:
                    nc.scalar.activation(
                        out=yn[:, t, 0 : TILES[n] * P],
                        in_=zT[:, 0 : TILES[n], :].rearrange("p j w -> p (j w)"),
                        func=ACT.Identity,
                        scale=gain[:, t : t + 1],
                        bias=bias[:, t : t + 1],
                    )

        def affine_on_vector(n):
            for t, zT in live["vector_banks", n]:
                nc.vector.tensor_scalar(
                    out=live["yn", n][:, t, 0 : TILES[n] * P],
                    in0=zT[:, 0 : TILES[n], :].rearrange("p j w -> p (j w)"),
                    scalar1=gain[:, t : t + 1],
                    scalar2=bias[:, t : t + 1],
                    op0=ALU.mult,
                    op1=ALU.add,
                )

        def transpose_tokens(n):
            x_sb = live["x_sb", n]
            x_grouped = work.tile([P, MAX_TOKENS * PACK], BF16, name="x_grouped", align_bytes=64)
            x_words = x_grouped[:].bitcast(F32).rearrange("p (j w u) -> p j w u", j=MAX_TILES, u=2)
            for first in range(0, TILES[n], 2):
                xT = psum.tile([P, 2, 2, P], F32, name="xT", tag="bank")
                for j in range(2):
                    for u in range(2):
                        nc.tensor.transpose(
                            xT[:, j, u, :], x_sb[:, first + j, :].bitcast(F32)[:, u : 2 * P : 2], ident_f32[:]
                        )
                nc.scalar.copy(out=x_words[:, first : first + 2], in_=xT[:].rearrange("p j u w -> p j w u"))
            live["x_grouped", n] = x_grouped

        def quantise_tokens(n):
            live["x_mx", n] = quantise(live["x_grouped", n][:, 0 : TILES[n] * P * PACK], work, "x")

        def gate(n):
            x_codes, x_scales = live["x_mx", n]
            wg_codes, wg_scales = live["wg_mx"]
            gated = work.tile([P, MAX_TILES, P // RUN, PACK, RUN], F32, name="gated")
            for j in range(TILES[n]):
                tokens = slice(j * P, (j + 1) * P)
                g_ps = psum.tile([P, PACK, P], F32, name="g_ps", tag="bank")
                for t in range(PACK):
                    slot = slice(t * P, (t + 1) * P)
                    nc.tensor.matmul_mx(
                        out=g_ps[:, t, :],
                        lhsT=wg_codes[:, slot].bitcast(FP8X4),
                        lhsT_scale=wg_scales[:, slot],
                        rhs=x_codes[:, tokens].bitcast(FP8X4),
                        rhs_scale=x_scales[:, tokens],
                        start=True,
                        stop=True,
                    )
                nc.scalar.activation(
                    out=gated[:, j], in_=g_ps[:].rearrange("p t (c i) -> p c t i", i=RUN), func=ACT.Silu
                )
            live["gated", n] = gated

        def multiply(n):
            hidden = work.tile([P, MAX_TOKENS, PACK], BF16, name="hidden", align_bytes=64)
            tokens = slice(0, TILES[n] * P)
            nc.vector.tensor_tensor(
                out=hidden[:, tokens, :].rearrange("p (c i) t -> p c t i", i=RUN),
                in0=live["gated", n][:, 0 : TILES[n]].rearrange("p j c t i -> p (j c) t i"),
                in1=live["yn", n][:, :, tokens].rearrange("p t (c i) -> p c t i", i=RUN),
                op=ALU.mult,
            )
            live["hidden", n] = hidden

        def quantise_hidden(n):
            hidden = live["hidden", n][:, 0 : TILES[n] * P, :]
            live["h_mx", n] = quantise(hidden.rearrange("p w t -> p (w t)"), work, "h")

        def project(n):
            h_codes, h_scales = live["h_mx", n]
            wp_codes, wp_scales = live["wp_mx"]
            out_sb = work.tile([P, MAX_TILES, WIDTH], F32, name="out_sb")
            for j in range(TILES[n]):
                tokens = slice(j * P, (j + 1) * P)
                o_ps = psum.tile([P, WIDTH], F32, name="o_ps", tag="bank")
                nc.tensor.matmul_mx(
                    out=o_ps[:],
                    lhsT=h_codes[:, tokens].bitcast(FP8X4),
                    lhsT_scale=h_scales[:, tokens],
                    rhs=wp_codes[:].bitcast(FP8X4),
                    rhs_scale=wp_scales[:],
                    start=True,
                    stop=True,
                )
                if n == GROUPS - 1 and j % 2 == 1:
                    nc.vector.tensor_copy(out=out_sb[:, j, :], in_=o_ps[:])
                else:
                    nc.scalar.copy(out=out_sb[:, j, :], in_=o_ps[:])
                nc.sync.dma_start(out=rows_of(out, n)[:, j, :], in_=out_sb[:, j, :])

        load(0)
        wg_raw = consts.tile([P, PACK, WIDTH], BF16, name="wg_raw")
        nc.sync.dma_start(out=wg_raw[:], in_=w_g.rearrange("(p t) c -> p t c", t=PACK))
        load_x(1)
        gain_raw = consts.tile([P, PACK], BF16, name="gain_raw")
        nc.sync.dma_start(out=gain_raw[:], in_=gn_weight.rearrange("(p t) -> p t", t=PACK))
        bias_raw = consts.tile([P, PACK], BF16, name="bias_raw")
        nc.sync.dma_start(out=bias_raw[:], in_=gn_bias.rearrange("(p t) -> p t", t=PACK))
        load_y(1)
        wp_raw = consts.tile([P, PACK, WIDTH], BF16, name="wp_raw")
        nc.sync.dma_start(out=wp_raw[:], in_=w_proj.rearrange("(p t) c -> p t c", t=PACK))
        for n in range(2, LOAD_AHEAD):
            load(n)
        wg_grouped = consts.tile([P, WIDTH, PACK], BF16, name="wg_grouped", align_bytes=64)
        wp_grouped = consts.tile([P, WIDTH, PACK], BF16, name="wp_grouped", align_bytes=64)

        ident_f32 = consts.tile([P, P], F32, name="ident_f32")
        make_identity(nc, ident_f32[:])
        minus_half = consts.tile([P, MAX_PAIRS], F32, name="minus_half")
        nc.vector.memset(minus_half[:], -0.5)
        gain = consts.tile([P, PACK], F32, name="gain")
        bias = consts.tile([P, PACK], F32, name="bias")
        table_warmer = consts.tile([P, 1], F32, name="table_warmer")
        nc.scalar.activation(out=table_warmer[:], in_=minus_half[:, 0:1], func=ACT.Silu)

        def run(stage, n):
            if 0 <= n < GROUPS:
                stage(n)

        for step in range(GROUPS + LAST_STAGE):
            run(affine_on_vector, step - 3)
            run(quantise_tokens, step - 1)
            if step == 1:
                nc.vector.tensor_copy(
                    out=wg_grouped[:].rearrange("p (t m) k -> p t m k", t=PACK),
                    in_=wg_raw[:].rearrange("p k (m t) -> p t m k", t=PACK),
                )
                live["wg_mx"] = quantise(wg_grouped[:].rearrange("p c k -> p (c k)"), consts, "wg")
                nc.vector.tensor_copy(out=gain[:], in_=gain_raw[:])
                nc.vector.tensor_copy(out=bias[:], in_=bias_raw[:])
            run(multiply, step - 3)
            run(project, step - 4)
            run(quantise_hidden, step - 3)
            run(statistics, step)
            if step == 0:
                inverse_roots(0)
            run(centre_and_scale, step - 1)
            if step == 2:
                live["wp_mx"] = quantise(wp_grouped[:].rearrange("p c k -> p (c k)"), consts, "wp")
            run(gate, step - 2)
            run(affine, step - 2)
            run(transpose_tokens, step)
            if step == 1:
                nc.scalar.copy(out=wp_grouped[:], in_=wp_raw[:].rearrange("p k c -> p c k"))
            run(load, step + LOAD_AHEAD)
